import numpy as np
import ml_dtypes


def mxq(x, axis, fmt="e4m3"):
    dtype, down = {"e4m3": (ml_dtypes.float8_e4m3fn, 7), "e5m2": (ml_dtypes.float8_e5m2, 14)}[fmt]
    v = np.moveaxis(np.asarray(x, np.float32).astype(ml_dtypes.bfloat16).astype(np.float64), axis, -1)
    blocks = v.reshape(v.shape[:-1] + (-1, 32))
    amax = np.abs(blocks).max(-1, keepdims=True)
    byte = np.maximum(np.where(amax > 0, np.frexp(amax)[1] - 1 + 127, 0) - down, 1)
    scale = np.exp2(byte - 127.0)
    codes = (blocks / scale).astype(np.float32).astype(dtype).astype(np.float64)
    return np.moveaxis((codes * scale).reshape(v.shape), -1, axis)


WIDE = False


def mx_kscale(k):
    if not WIDE:
        return np.ones(k)
    levels = np.array([10, -10, 5, -5, 0])
    a = np.random.permutation(np.resize(levels, k // 512 * 4)).reshape(k // 512, 4)
    idx = np.arange(k)
    return np.exp2(a[idx // 512, idx % 128 // 32])


BF16 = ml_dtypes.bfloat16


def bf(x):
    return np.asarray(x, np.float32).astype(BF16)


def f64(x):
    return np.asarray(x).astype(np.float64)


E2M1 = np.array([0.0, 0.5, 1.0, 1.5, 2.0, 3.0, 4.0, 6.0, -0.0, -0.5, -1.0, -1.5, -2.0, -3.0, -4.0, -6.0])


def pack_weight(w, fmt):
    k, n = w.shape
    w = f64(bf(w)).reshape(k // 32, 32, n)
    amax = np.abs(w).max(1)
    if fmt == "e4m3":
        byte = np.frexp(amax)[1] - 1 + 127 - 7
    else:
        mant, ex = np.frexp(amax / 6.0)
        byte = np.where(mant > 0.5, ex, ex - 1) + 127
    byte = np.clip(np.where(amax > 0, byte, 1), 1, 254)
    scaled = (w * np.exp2(127.0 - byte)[:, None, :]).reshape(k, n).astype(np.float32)
    by_word = np.ascontiguousarray(scaled.reshape(k // 512, 128, 4, n).transpose(0, 1, 3, 2))
    if fmt == "e4m3":
        words = by_word.astype(ml_dtypes.float8_e4m3fn).view(np.uint8)
    else:
        c = by_word.astype(ml_dtypes.float4_e2m1fn).view(np.uint8) & 0xF
        words = c[..., 0::2] | (c[..., 1::2] << 4)
    return np.ascontiguousarray(words), np.ascontiguousarray(byte.astype(np.uint8).reshape(k // 512, 16, n))


def unpack_weight(words, scales, fmt):
    g, p, n, _ = words.shape
    if fmt == "e4m3":
        vals = np.ascontiguousarray(words).view(ml_dtypes.float8_e4m3fn).astype(np.float64)
    else:
        nib = np.empty((g, p, n, 4), np.uint8)
        nib[..., 0::2] = words & 0xF
        nib[..., 1::2] = words >> 4
        vals = E2M1[nib]
    vals = vals * np.repeat(np.exp2(scales.astype(np.float64) - 127.0), 8, axis=1)[..., None]
    return vals.transpose(0, 1, 3, 2).reshape(g * 512, n)


B, IN, H = 128, 8192, 512
G = 4 * H
EPS = 1e-5
FMT = "e4m3"


def _layernorm(v, gamma, beta):
    mean = np.mean(v, axis=-1, keepdims=True)
    var = np.mean(np.square(v - mean), axis=-1, keepdims=True)
    return (v - mean) / np.sqrt(var + EPS) * gamma + beta


def sigmoid(v):
    return 1.0 / (1.0 + np.exp(-v))


def setup_inputs():
    s, t = mx_kscale(IN), mx_kscale(H)
    x = bf(np.random.standard_normal((B, IN)) * s)
    h_prev = bf(np.random.standard_normal((B, H)) * t)
    c_prev = bf(np.random.standard_normal((B, H)))
    W_ih_words, W_ih_scales = pack_weight(np.random.standard_normal((IN, G)) / np.sqrt(IN) / s[:, None], FMT)
    W_hh_words, W_hh_scales = pack_weight(np.random.standard_normal((H, G)) / np.sqrt(H) / t[:, None], FMT)
    return {
        "x": x,
        "h_prev": h_prev,
        "c_prev": c_prev,
        "W_ih_words": W_ih_words,
        "W_ih_scales": W_ih_scales,
        "W_hh_words": W_hh_words,
        "W_hh_scales": W_hh_scales,
        "gamma_ih": bf(1.0 + 0.2 * np.random.standard_normal(G)),
        "beta_ih": bf(0.3 * np.random.standard_normal(G)),
        "gamma_hh": bf(1.0 + 0.2 * np.random.standard_normal(G)),
        "beta_hh": bf(0.3 * np.random.standard_normal(G)),
        "gamma_c": bf(1.0 + 0.2 * np.random.standard_normal(H)),
        "beta_c": bf(0.3 * np.random.standard_normal(H)),
    }


def reference(x, h_prev, c_prev, W_ih_words, W_ih_scales, W_hh_words, W_hh_scales, gamma_ih, beta_ih, gamma_hh, beta_hh, gamma_c, beta_c):
    a_ih = mxq(f64(x), 1, "e4m3") @ unpack_weight(W_ih_words, W_ih_scales, FMT)
    a_hh = mxq(f64(h_prev), 1, "e4m3") @ unpack_weight(W_hh_words, W_hh_scales, FMT)
    gates_ih = _layernorm(a_ih, f64(gamma_ih), f64(beta_ih))
    gates_hh = _layernorm(a_hh, f64(gamma_hh), f64(beta_hh))
    gates = gates_ih + gates_hh
    i_g, f_g, g_g, o_g = np.split(gates, 4, axis=1)
    i_t = sigmoid(i_g)
    f_t = sigmoid(f_g)
    g_t = np.tanh(g_g)
    o_t = sigmoid(o_g)
    c_t = f_t * f64(c_prev) + i_t * g_t
    h_t = o_t * np.tanh(_layernorm(c_t, f64(gamma_c), f64(beta_c)))
    return (h_t, c_t)

@@ -1,0 +1,296 @@
+from contextlib import ExitStack
+
+import concourse.mybir as mybir
+from concourse.masks import make_identity
+
+F32 = mybir.dt.float32
+BF16 = mybir.dt.bfloat16
+I32 = mybir.dt.int32
+U32 = mybir.dt.uint32
+U8 = mybir.dt.uint8
+FP8X4 = mybir.dt.float8_e4m3fn_x4
+ALU = mybir.AluOpType
+ACT = mybir.ActivationFunctionType
+
+P = 128
+PACK = 4
+K_PASS = P * PACK
+IN = 8192
+H = 512
+GATES = 4
+GATE_I, GATE_F, GATE_G, GATE_O = 0, 1, 2, 3
+EPS = 1e-5
+IH_PASSES = IN // K_PASS
+HH_PASS = IH_PASSES
+WORDS = K_PASS // 2
+PLANES_IN_TILE = 4
+X_LOADS = 4
+BN_STATS = 6
+LATE_PASSES = 2
+EARLY_PASSES = IH_PASSES - LATE_PASSES
+
+FLOPS = 2 * P * (IN + H) * GATES * H
+
+
+def gate_cols(n):
+    return slice(H * n, H * (n + 1))
+
+
+def tile_layernormlstmcell_k_kernel(
+    tc,
+    x,
+    h_prev,
+    c_prev,
+    W_ih_words,
+    W_ih_scales,
+    W_hh_words,
+    W_hh_scales,
+    gamma_ih,
+    beta_ih,
+    gamma_hh,
+    beta_hh,
+    gamma_c,
+    beta_c,
+    out_0,
+    out_1,
+):
+    nc = tc.nc
+    with ExitStack() as ctx:
+        keep = ctx.enter_context(tc.tile_pool(name="keep", bufs=1))
+        stage = ctx.enter_context(tc.tile_pool(name="stage", bufs=2))
+        ih_banks = ctx.enter_context(tc.psum_pool(name="ih_banks", bufs=1))
+        lent_banks = ctx.enter_context(tc.psum_pool(name="lent_banks", bufs=4))
+        ctx.enter_context(tc.manual_schedule())
+
+        warm = keep.tile([P, 1], F32)
+        neg_half = keep.tile([P, 1], F32)
+        ones = keep.tile([P, P], BF16)
+        ident = keep.tile([P, P], F32)
+        nc.vector.memset(warm[:], 0.0)
+        nc.vector.memset(neg_half[:], -0.5)
+        nc.vector.memset(ones[:], 1.0)
+        make_identity(nc, ident[:])
+
+        plane_tiles = IH_PASSES // PLANES_IN_TILE + 1
+        planes = keep.tile([P, plane_tiles, GATES * H], U8, align_bytes=64)
+        nc.vector.memset(planes[:].bitcast(I32), 0)
+
+        col_gamma_hh, col_gamma_ih = 0, GATES * H
+        col_gamma_c, col_beta_c = 2 * GATES * H, 2 * GATES * H + H
+        col_beta = 2 * GATES * H + 2 * H
+        vec_cols = col_beta + GATES * H
+        vec_rows = keep.tile([P, vec_cols], BF16)
+        nc.vector.memset(vec_rows[:], 0.0)
+
+        h_sb = keep.tile([P, H], BF16)
+        c_sb = keep.tile([P, H], BF16)
+        nc.scalar.dma_start(out=h_sb[:], in_=h_prev)
+        nc.scalar.dma_start(out=c_sb[:], in_=c_prev)
+        nc.scalar.activation(out=warm[:], in_=warm[:], func=ACT.Sigmoid)
+        for vector, row, col in (
+            (gamma_hh, 0, col_gamma_hh),
+            (beta_ih, 0, col_beta),
+            (beta_hh, 1, col_beta),
+            (gamma_ih, 0, col_gamma_ih),
+            (gamma_c, 0, col_gamma_c),
+            (beta_c, 0, col_beta_c),
+        ):
+            nc.scalar.dma_start(
+                out=vec_rows[row : row + 1, col : col + vector.shape[0]],
+                in_=vector.rearrange("(o n) -> o n", o=1),
+            )
+
+        x_sb = keep.tile([P, IN], BF16)
+        x_piece = IN // X_LOADS
+        for i in range(X_LOADS):
+            cols = slice(x_piece * i, x_piece * (i + 1))
+            nc.sync.dma_start(out=x_sb[:, cols], in_=x[:, cols])
+
+        for Q in range(4):
+            nc.sync.dma_start(
+                out=planes[32 * Q : 32 * Q + 4, plane_tiles - 1, :].bitcast(I32),
+                in_=W_hh_scales[0, 4 * Q : 4 * Q + 4, :].bitcast(I32),
+            )
+        for j in range(IH_PASSES // PLANES_IN_TILE):
+            for Q in range(4):
+                nc.sync.dma_start(
+                    out=planes[32 * Q : 32 * Q + 16, j, :].bitcast(I32),
+                    in_=W_ih_scales[
+                        PLANES_IN_TILE * j : PLANES_IN_TILE * (j + 1), 4 * Q : 4 * Q + 4, :
+                    ].bitcast(I32),
+                )
+
+        w_hh = keep.tile([P, GATES * H], I32, align_bytes=64)
+        nc.sync.dma_start(
+            out=w_hh[:], in_=W_hh_words[0].rearrange("p n t -> p (n t)").bitcast(I32)
+        )
+        w_early = []
+        for g in range(EARLY_PASSES):
+            w_pass = keep.tile([P, GATES * H], I32, name="w_pass%d" % g, align_bytes=64)
+            nc.sync.dma_start(
+                out=w_pass[:], in_=W_ih_words[g].rearrange("p n t -> p (n t)").bitcast(I32)
+            )
+            w_early.append(w_pass)
+        w_late = []
+        late_bytes = W_ih_words[EARLY_PASSES:IH_PASSES].rearrange("g p n t -> p g (n t)")
+        for n in range(GATES):
+            w_gate = keep.tile([P, LATE_PASSES, H], I32, name="w_gate%d" % n, align_bytes=64)
+            nc.sync.dma_start(
+                out=w_gate[:],
+                in_=late_bytes[:, :, PACK * H * n : PACK * H * (n + 1)].bitcast(I32),
+            )
+            w_late.append(w_gate)
+
+        act_codes = keep.tile([P, (IH_PASSES + 1) * P], U32, align_bytes=64)
+        act_scales = keep.tile([P, (IH_PASSES + 1) * P], U8, align_bytes=64)
+
+        def quantise_passes(rows, first_pass, passes):
+            words = rows.bitcast(F32)
+            turned = lent_banks.tile([P, passes, 2, P], F32, tag="lent")
+            for g in range(passes):
+                for u in range(2):
+                    nc.tensor.transpose(
+                        turned[:, g, u, :], words[:, WORDS * g + u : WORDS * (g + 1) : 2], ident[:]
+                    )
+            grouped = stage.tile([P, passes * K_PASS], BF16, tag="grouped", align_bytes=64)
+            nc.scalar.copy(
+                out=grouped[:].bitcast(F32).rearrange("p (g b u) -> p g b u", g=passes, u=2),
+                in_=turned[:].rearrange("p g u b -> p g b u"),
+            )
+            cols = slice(P * first_pass, P * (first_pass + passes))
+            nc.vector.quantize_mx(
+                out=act_codes[:, cols].bitcast(FP8X4), scales=act_scales[:, cols], in_=grouped[:]
+            )
+
+        quantise_passes(h_sb[:], HH_PASS, 1)
+        for g in range(0, IH_PASSES, 2):
+            quantise_passes(x_sb[:, K_PASS * g : K_PASS * (g + 2)], g, 2)
+
+        spread = keep.tile([P, col_beta], BF16)
+        hh_term = keep.tile([P, GATES * H], F32)
+        for block in range(vec_cols // H):
+            cols = slice(H * block, H * (block + 1))
+            summed = lent_banks.tile([P, H], F32, tag="lent")
+            nc.tensor.matmul(out=summed[:], lhsT=ones[:], rhs=vec_rows[:, cols], start=True, stop=True)
+            if H * block < col_beta:
+                target = spread[:, cols]
+            else:
+                target = hh_term[:, H * block - col_beta : H * (block + 1) - col_beta]
+            if block % 2 == 0:
+                nc.scalar.copy(out=target, in_=summed[:])
+            else:
+                nc.vector.tensor_copy(out=target, in_=summed[:])
+        gamma_hh_all = spread[:, col_gamma_hh : col_gamma_hh + GATES * H]
+        gamma_ih_all = spread[:, col_gamma_ih : col_gamma_ih + GATES * H]
+        gamma_c_all = spread[:, col_gamma_c : col_gamma_c + H]
+        beta_c_all = spread[:, col_beta_c : col_beta_c + H]
+
+        def mean_and_inverse_std(stats, label):
+            mean_var = keep.tile([P, 2], F32, name="mean_var_" + label)
+            var_eps = keep.tile([P, 1], F32, name="var_eps_" + label)
+            inv_std = keep.tile([P, 1], F32, name="inv_std_" + label)
+            nc.vector.bn_aggr(out=mean_var[:], in_=stats[:].rearrange("p r s -> p (r s)"))
+            nc.vector.tensor_scalar_add(out=var_eps[:], in0=mean_var[:, 1:2], scalar1=EPS)
+            nc.gpsimd.tensor_tensor(out=inv_std[:], in0=var_eps[:], in1=neg_half[:], op=ALU.pow)
+            return mean_var[:, 0:1], inv_std[:]
+
+        def centre(out, in_, mean, gamma):
+            nc.vector.scalar_tensor_tensor(
+                out=out, in0=in_, scalar=mean, in1=gamma, op0=ALU.subtract, op1=ALU.mult
+            )
+
+        def scale_and_add(out, in_, inv_std, addend):
+            nc.vector.scalar_tensor_tensor(
+                out=out, in0=in_, scalar=inv_std, in1=addend, op0=ALU.mult, op1=ALU.add
+            )
+
+        gate = keep.tile([P, GATES * H], F32)
+
+        hh_cols = slice(P * HH_PASS, P * (HH_PASS + 1))
+        hh_stats = keep.tile([P, GATES, BN_STATS], F32)
+        hh_acc = []
+        for n in range(GATES):
+            acc = lent_banks.tile([P, H], F32, name="hh_acc%d" % n, tag="lent")
+            nc.tensor.matmul_mx(
+                out=acc[:],
+                lhsT=act_codes[:, hh_cols].bitcast(FP8X4),
+                lhsT_scale=act_scales[:, hh_cols],
+                rhs=w_hh[:, gate_cols(n)].bitcast(FP8X4),
+                rhs_scale=planes[:, plane_tiles - 1, gate_cols(n)],
+                start=True,
+                stop=True,
+            )
+            nc.vector.bn_stats(out=hh_stats[:, n, :], in_=acc[:])
+            hh_acc.append(acc)
+        hh_mean, hh_inv_std = mean_and_inverse_std(hh_stats, "hh")
+        for n in range(GATES):
+            centre(gate[:, gate_cols(n)], hh_acc[n][:], hh_mean, gamma_hh_all[:, gate_cols(n)])
+        for n in range(GATES):
+            scale_and_add(
+                hh_term[:, gate_cols(n)], gate[:, gate_cols(n)], hh_inv_std, hh_term[:, gate_cols(n)]
+            )
+
+        ih_acc = []
+        for n in range(GATES):
+            acc = ih_banks.tile([P, H], F32, name="ih_acc%d" % n)
+            ih_acc.append(acc)
+
+        def ih_pass(n, g, words):
+            plane_tile, place = divmod(g, PLANES_IN_TILE)
+            cols = slice(P * g, P * (g + 1))
+            nc.tensor.matmul_mx(
+                out=ih_acc[n][:],
+                lhsT=act_codes[:, cols].bitcast(FP8X4),
+                lhsT_scale=act_scales[:, cols],
+                rhs=words.bitcast(FP8X4),
+                rhs_scale=planes[4 * place : P, plane_tile, gate_cols(n)],
+                start=(g == 0),
+                stop=(g == IH_PASSES - 1),
+            )
+
+        for g in range(EARLY_PASSES):
+            for n in range(GATES):
+                ih_pass(n, g, w_early[g][:, gate_cols(n)])
+        ih_stats = keep.tile([P, GATES, BN_STATS], F32)
+        for n in range(GATES):
+            for late in range(LATE_PASSES):
+                ih_pass(n, EARLY_PASSES + late, w_late[n][:, late, :])
+            nc.vector.bn_stats(out=ih_stats[:, n, :], in_=ih_acc[n][:])
+
+        ih_mean, ih_inv_std = mean_and_inverse_std(ih_stats, "ih")
+
+        def centre_gate(n):
+            centre(gate[:, gate_cols(n)], ih_acc[n][:], ih_mean, gamma_ih_all[:, gate_cols(n)])
+
+        def finish_gate(n, func):
+            cols = gate_cols(n)
+            scale_and_add(gate[:, cols], gate[:, cols], ih_inv_std, hh_term[:, cols])
+            nc.scalar.activation(out=gate[:, cols], in_=gate[:, cols], func=func)
+
+        centre_gate(GATE_G)
+        centre_gate(GATE_I)
+        finish_gate(GATE_G, ACT.Tanh)
+        finish_gate(GATE_I, ACT.Sigmoid)
+        centre_gate(GATE_F)
+        centre_gate(GATE_O)
+        finish_gate(GATE_F, ACT.Sigmoid)
+
+        new_part = keep.tile([P, H], F32)
+        kept_part = keep.tile([P, H], F32)
+        c_t = keep.tile([P, H], F32)
+        nc.vector.tensor_mul(out=new_part[:], in0=gate[:, gate_cols(GATE_I)], in1=gate[:, gate_cols(GATE_G)])
+        nc.vector.tensor_mul(out=kept_part[:], in0=gate[:, gate_cols(GATE_F)], in1=c_sb[:])
+        nc.vector.tensor_add(out=c_t[:], in0=new_part[:], in1=kept_part[:])
+        nc.sync.dma_start(out=out_1, in_=c_t[:])
+
+        c_stats = keep.tile([P, 1, BN_STATS], F32)
+        nc.vector.bn_stats(out=c_stats[:, 0, :], in_=c_t[:])
+        c_mean, c_inv_std = mean_and_inverse_std(c_stats, "c")
+        c_norm = keep.tile([P, H], F32)
+        h_t = keep.tile([P, H], F32)
+        centre(c_norm[:], c_t[:], c_mean, gamma_c_all)
+        finish_gate(GATE_O, ACT.Sigmoid)
+        scale_and_add(c_norm[:], c_norm[:], c_inv_std, beta_c_all)
+        nc.scalar.activation(out=c_norm[:], in_=c_norm[:], func=ACT.Tanh)
+        nc.vector.tensor_mul(out=h_t[:], in0=gate[:, gate_cols(GATE_O)], in1=c_norm[:])
+        nc.sync.dma_start(out=out_0, in_=h_t[:])

@@ -64,47 +64,48 @@ def tile_layernormlstmcell_k_kernel(
 
         warm = keep.tile([P, 1], F32)
         neg_half = keep.tile([P, 1], F32)
-        ones = keep.tile([P, P], BF16)
+        ident_bf = keep.tile([P, P], BF16)
         ident = keep.tile([P, P], F32)
         nc.vector.memset(warm[:], 0.0)
         nc.vector.memset(neg_half[:], -0.5)
-        nc.vector.memset(ones[:], 1.0)
         make_identity(nc, ident[:])
 
         plane_tiles = IH_PASSES // PLANES_IN_TILE + 1
         planes = keep.tile([P, plane_tiles, GATES * H], U8, align_bytes=64)
-        nc.vector.memset(planes[:].bitcast(I32), 0)
+        nc.vector.memset(planes[:, plane_tiles - 1, :].bitcast(I32), 0)
+        for j in range(plane_tiles - 1):
+            nc.vector.memset(planes[:, j, :].bitcast(I32), 0)
 
-        col_gamma_hh, col_gamma_ih = 0, GATES * H
-        col_gamma_c, col_beta_c = 2 * GATES * H, 2 * GATES * H + H
-        col_beta = 2 * GATES * H + 2 * H
-        vec_cols = col_beta + GATES * H
-        vec_rows = keep.tile([P, vec_cols], BF16)
-        nc.vector.memset(vec_rows[:], 0.0)
-
-        h_sb = keep.tile([P, H], BF16)
-        c_sb = keep.tile([P, H], BF16)
-        nc.scalar.dma_start(out=h_sb[:], in_=h_prev)
-        nc.scalar.dma_start(out=c_sb[:], in_=c_prev)
-        nc.scalar.activation(out=warm[:], in_=warm[:], func=ACT.Sigmoid)
-        for vector, row, col in (
-            (gamma_hh, 0, col_gamma_hh),
-            (beta_ih, 0, col_beta),
-            (beta_hh, 1, col_beta),
-            (gamma_ih, 0, col_gamma_ih),
-            (gamma_c, 0, col_gamma_c),
-            (beta_c, 0, col_beta_c),
-        ):
-            nc.scalar.dma_start(
-                out=vec_rows[row : row + 1, col : col + vector.shape[0]],
-                in_=vector.rearrange("(o n) -> o n", o=1),
-            )
+        row_gamma_hh, row_gamma_ih, row_beta_ih, row_beta_hh = 0, GATES, 2 * GATES, 3 * GATES
+        row_gamma_c, row_beta_c = 4 * GATES, 4 * GATES + 1
+        vec_rows = keep.tile([P, H], BF16)
+        nc.vector.memset(vec_rows[:].bitcast(I32), 0)
+        nc.vector.tensor_copy(out=ident_bf[:], in_=ident[:])
 
         x_sb = keep.tile([P, IN], BF16)
         x_piece = IN // X_LOADS
         for i in range(X_LOADS):
             cols = slice(x_piece * i, x_piece * (i + 1))
             nc.sync.dma_start(out=x_sb[:, cols], in_=x[:, cols])
+
+        h_sb = keep.tile([P, H], BF16)
+        c_sb = keep.tile([P, H], BF16)
+        nc.scalar.dma_start(out=h_sb[:], in_=h_prev)
+        nc.scalar.activation(out=warm[:], in_=warm[:], func=ACT.Sigmoid)
+        for vector, row in (
+            (gamma_hh, row_gamma_hh),
+            (gamma_ih, row_gamma_ih),
+            (beta_ih, row_beta_ih),
+            (beta_hh, row_beta_hh),
+            (gamma_c, row_gamma_c),
+            (beta_c, row_beta_c),
+        ):
+            rows = vector.shape[0] // H
+            nc.scalar.dma_start(
+                out=vec_rows[row : row + rows, :], in_=vector.rearrange("(r n) -> r n", r=rows)
+            )
+        nc.scalar.dma_start(out=c_sb[:], in_=c_prev)
+
 
         for Q in range(4):
             nc.sync.dma_start(
@@ -166,24 +167,36 @@ def tile_layernormlstmcell_k_kernel(
         for g in range(0, IH_PASSES, 2):
             quantise_passes(x_sb[:, K_PASS * g : K_PASS * (g + 2)], g, 2)
 
-        spread = keep.tile([P, col_beta], BF16)
+        def spread_rows(rows_to_add, target, engine_copy):
+            summed = lent_banks.tile([P, H], F32, name="summed", tag="lent")
+            for i, r in enumerate(rows_to_add):
+                nc.tensor.matmul(
+                    out=summed[:],
+                    lhsT=ident_bf[:, r : r + 1].to_broadcast([P, P]),
+                    rhs=vec_rows[:],
+                    start=(i == 0),
+                    stop=(i == len(rows_to_add) - 1),
+                )
+            engine_copy(out=target, in_=summed[:])
+
+        gamma_hh_all = keep.tile([P, GATES * H], BF16)
+        gamma_ih_all = keep.tile([P, GATES * H], BF16)
+        gamma_c_all = keep.tile([P, H], BF16)
+        beta_c_all = keep.tile([P, H], BF16)
         hh_term = keep.tile([P, GATES * H], F32)
-        for block in range(vec_cols // H):
-            cols = slice(H * block, H * (block + 1))
-            summed = lent_banks.tile([P, H], F32, tag="lent")
-            nc.tensor.matmul(out=summed[:], lhsT=ones[:], rhs=vec_rows[:, cols], start=True, stop=True)
-            if H * block < col_beta:
-                target = spread[:, cols]
-            else:
-                target = hh_term[:, H * block - col_beta : H * (block + 1) - col_beta]
-            if block % 2 == 0:
-                nc.scalar.copy(out=target, in_=summed[:])
-            else:
-                nc.vector.tensor_copy(out=target, in_=summed[:])
-        gamma_hh_all = spread[:, col_gamma_hh : col_gamma_hh + GATES * H]
-        gamma_ih_all = spread[:, col_gamma_ih : col_gamma_ih + GATES * H]
-        gamma_c_all = spread[:, col_gamma_c : col_gamma_c + H]
-        beta_c_all = spread[:, col_beta_c : col_beta_c + H]
+        for n in range(GATES):
+            spread_rows([row_gamma_hh + n], gamma_hh_all[:, gate_cols(n)], nc.scalar.copy)
+            spread_rows(
+                [row_beta_ih + n, row_beta_hh + n], hh_term[:, gate_cols(n)], nc.vector.tensor_copy
+            )
+        for n in range(GATES):
+            spread_rows(
+                [row_gamma_ih + n],
+                gamma_ih_all[:, gate_cols(n)],
+                nc.scalar.copy if n % 2 == 0 else nc.vector.tensor_copy,
+            )
+        spread_rows([row_gamma_c], gamma_c_all[:], nc.scalar.copy)
+        spread_rows([row_beta_c], beta_c_all[:], nc.vector.tensor_copy)
 
         def mean_and_inverse_std(stats, label):
             mean_var = keep.tile([P, 2], F32, name="mean_var_" + label)
@@ -288,9 +301,9 @@ def tile_layernormlstmcell_k_kernel(
         c_mean, c_inv_std = mean_and_inverse_std(c_stats, "c")
         c_norm = keep.tile([P, H], F32)
         h_t = keep.tile([P, H], F32)
-        centre(c_norm[:], c_t[:], c_mean, gamma_c_all)
+        centre(c_norm[:], c_t[:], c_mean, gamma_c_all[:])
         finish_gate(GATE_O, ACT.Sigmoid)
-        scale_and_add(c_norm[:], c_norm[:], c_inv_std, beta_c_all)
+        scale_and_add(c_norm[:], c_norm[:], c_inv_std, beta_c_all[:])
         nc.scalar.activation(out=c_norm[:], in_=c_norm[:], func=ACT.Tanh)
         nc.vector.tensor_mul(out=h_t[:], in0=gate[:, gate_cols(GATE_O)], in1=c_norm[:])
         nc.sync.dma_start(out=out_0, in_=h_t[:])

@@ -106,20 +106,25 @@ def tile_layernormlstmcell_k_kernel(
             )
         nc.scalar.dma_start(out=c_sb[:], in_=c_prev)
 
-
-        for Q in range(4):
-            nc.sync.dma_start(
-                out=planes[32 * Q : 32 * Q + 4, plane_tiles - 1, :].bitcast(I32),
-                in_=W_hh_scales[0, 4 * Q : 4 * Q + 4, :].bitcast(I32),
-            )
-        for j in range(IH_PASSES // PLANES_IN_TILE):
+        def load_hh_scales():
             for Q in range(4):
-                nc.sync.dma_start(
-                    out=planes[32 * Q : 32 * Q + 16, j, :].bitcast(I32),
+                nc.gpsimd.dma_start(
+                    out=planes[32 * Q : 32 * Q + 4, plane_tiles - 1, :].bitcast(F32),
+                    in_=W_hh_scales[0, 4 * Q : 4 * Q + 4, :].bitcast(F32),
+                )
+
+        def load_ih_scales(j):
+            for Q in range(4):
+                nc.gpsimd.dma_start(
+                    out=planes[32 * Q : 32 * Q + 16, j, :].bitcast(F32),
                     in_=W_ih_scales[
                         PLANES_IN_TILE * j : PLANES_IN_TILE * (j + 1), 4 * Q : 4 * Q + 4, :
-                    ].bitcast(I32),
+                    ].bitcast(F32),
                 )
+
+        load_hh_scales()
+        for j in range(IH_PASSES // PLANES_IN_TILE):
+            load_ih_scales(j)
 
         w_hh = keep.tile([P, GATES * H], I32, align_bytes=64)
         nc.sync.dma_start(

@@ -172,7 +172,7 @@ def tile_layernormlstmcell_k_kernel(
         for g in range(0, IH_PASSES, 2):
             quantise_passes(x_sb[:, K_PASS * g : K_PASS * (g + 2)], g, 2)
 
-        def spread_rows(rows_to_add, target, engine_copy):
+        def spread_rows(rows_to_add):
             summed = lent_banks.tile([P, H], F32, name="summed", tag="lent")
             for i, r in enumerate(rows_to_add):
                 nc.tensor.matmul(
@@ -182,26 +182,23 @@ def tile_layernormlstmcell_k_kernel(
                     start=(i == 0),
                     stop=(i == len(rows_to_add) - 1),
                 )
-            engine_copy(out=target, in_=summed[:])
+            return summed
 
         gamma_hh_all = keep.tile([P, GATES * H], BF16)
         gamma_ih_all = keep.tile([P, GATES * H], BF16)
-        gamma_c_all = keep.tile([P, H], BF16)
-        beta_c_all = keep.tile([P, H], BF16)
         hh_term = keep.tile([P, GATES * H], F32)
         for n in range(GATES):
-            spread_rows([row_gamma_hh + n], gamma_hh_all[:, gate_cols(n)], nc.scalar.copy)
-            spread_rows(
-                [row_beta_ih + n, row_beta_hh + n], hh_term[:, gate_cols(n)], nc.vector.tensor_copy
+            nc.scalar.copy(out=gamma_hh_all[:, gate_cols(n)], in_=spread_rows([row_gamma_hh + n])[:])
+            nc.vector.tensor_copy(
+                out=hh_term[:, gate_cols(n)], in_=spread_rows([row_beta_ih + n, row_beta_hh + n])[:]
             )
         for n in range(GATES):
-            spread_rows(
-                [row_gamma_ih + n],
-                gamma_ih_all[:, gate_cols(n)],
-                nc.scalar.copy if n % 2 == 0 else nc.vector.tensor_copy,
-            )
-        spread_rows([row_gamma_c], gamma_c_all[:], nc.scalar.copy)
-        spread_rows([row_beta_c], beta_c_all[:], nc.vector.tensor_copy)
+            if n % 2 == 0:
+                nc.scalar.copy(out=gamma_ih_all[:, gate_cols(n)], in_=spread_rows([row_gamma_ih + n])[:])
+            else:
+                nc.vector.tensor_copy(
+                    out=gamma_ih_all[:, gate_cols(n)], in_=spread_rows([row_gamma_ih + n])[:]
+                )
 
         def mean_and_inverse_std(stats, label):
             mean_var = keep.tile([P, 2], F32, name="mean_var_" + label)
@@ -248,6 +245,9 @@ def tile_layernormlstmcell_k_kernel(
                 hh_term[:, gate_cols(n)], gate[:, gate_cols(n)], hh_inv_std, hh_term[:, gate_cols(n)]
             )
 
+        gamma_c_all = spread_rows([row_gamma_c])
+        beta_c_all = spread_rows([row_beta_c])
+
         ih_acc = []
         for n in range(GATES):
             acc = ih_banks.tile([P, H], F32, name="ih_acc%d" % n)
@@ -275,40 +275,70 @@ def tile_layernormlstmcell_k_kernel(
                 ih_pass(n, EARLY_PASSES + late, w_late[n][:, late, :])
             nc.vector.bn_stats(out=ih_stats[:, n, :], in_=ih_acc[n][:])
 
+        halves = 2
+        half = H // halves
+
+        def half_cols(n, i):
+            return slice(H * n + half * i, H * n + half * (i + 1))
+
         ih_mean, ih_inv_std = mean_and_inverse_std(ih_stats, "ih")
 
         def centre_gate(n):
-            centre(gate[:, gate_cols(n)], ih_acc[n][:], ih_mean, gamma_ih_all[:, gate_cols(n)])
+            for i in range(halves):
+                cols = half_cols(n, i)
+                centre(
+                    gate[:, cols], ih_acc[n][:, half_cols(0, i)], ih_mean, gamma_ih_all[:, cols]
+                )
 
         def finish_gate(n, func):
-            cols = gate_cols(n)
-            scale_and_add(gate[:, cols], gate[:, cols], ih_inv_std, hh_term[:, cols])
-            nc.scalar.activation(out=gate[:, cols], in_=gate[:, cols], func=func)
+            for i in range(halves):
+                cols = half_cols(n, i)
+                scale_and_add(gate[:, cols], gate[:, cols], ih_inv_std, hh_term[:, cols])
+                nc.scalar.activation(out=gate[:, cols], in_=gate[:, cols], func=func)
 
         centre_gate(GATE_G)
         centre_gate(GATE_I)
+        centre_gate(GATE_F)
         finish_gate(GATE_G, ACT.Tanh)
         finish_gate(GATE_I, ACT.Sigmoid)
-        centre_gate(GATE_F)
-        centre_gate(GATE_O)
         finish_gate(GATE_F, ACT.Sigmoid)
 
         new_part = keep.tile([P, H], F32)
         kept_part = keep.tile([P, H], F32)
         c_t = keep.tile([P, H], F32)
-        nc.vector.tensor_mul(out=new_part[:], in0=gate[:, gate_cols(GATE_I)], in1=gate[:, gate_cols(GATE_G)])
-        nc.vector.tensor_mul(out=kept_part[:], in0=gate[:, gate_cols(GATE_F)], in1=c_sb[:])
-        nc.vector.tensor_add(out=c_t[:], in0=new_part[:], in1=kept_part[:])
+        c_stats = keep.tile([P, halves, BN_STATS], F32)
+        for i in range(halves):
+            cols = half_cols(0, i)
+            nc.vector.tensor_mul(
+                out=new_part[:, cols], in0=gate[:, half_cols(GATE_I, i)], in1=gate[:, half_cols(GATE_G, i)]
+            )
+        for i in range(halves):
+            cols = half_cols(0, i)
+            nc.vector.tensor_mul(
+                out=kept_part[:, cols], in0=gate[:, half_cols(GATE_F, i)], in1=c_sb[:, cols]
+            )
+        for i in range(halves):
+            cols = half_cols(0, i)
+            nc.vector.tensor_add(out=c_t[:, cols], in0=new_part[:, cols], in1=kept_part[:, cols])
         nc.sync.dma_start(out=out_1, in_=c_t[:])
 
-        c_stats = keep.tile([P, 1, BN_STATS], F32)
-        nc.vector.bn_stats(out=c_stats[:, 0, :], in_=c_t[:])
+        for i in range(halves):
+            nc.vector.bn_stats(out=c_stats[:, i, :], in_=c_t[:, half_cols(0, i)])
         c_mean, c_inv_std = mean_and_inverse_std(c_stats, "c")
         c_norm = keep.tile([P, H], F32)
         h_t = keep.tile([P, H], F32)
-        centre(c_norm[:], c_t[:], c_mean, gamma_c_all[:])
+        centre_gate(GATE_O)
+        for i in range(halves):
+            cols = half_cols(0, i)
+            centre(c_norm[:, cols], c_t[:, cols], c_mean, gamma_c_all[:, cols])
         finish_gate(GATE_O, ACT.Sigmoid)
-        scale_and_add(c_norm[:], c_norm[:], c_inv_std, beta_c_all[:])
-        nc.scalar.activation(out=c_norm[:], in_=c_norm[:], func=ACT.Tanh)
-        nc.vector.tensor_mul(out=h_t[:], in0=gate[:, gate_cols(GATE_O)], in1=c_norm[:])
-        nc.sync.dma_start(out=out_0, in_=h_t[:])
+        for i in range(halves):
+            cols = half_cols(0, i)
+            scale_and_add(c_norm[:, cols], c_norm[:, cols], c_inv_std, beta_c_all[:, cols])
+            nc.scalar.activation(out=c_norm[:, cols], in_=c_norm[:, cols], func=ACT.Tanh)
+        for i in range(halves):
+            cols = half_cols(0, i)
+            nc.vector.tensor_mul(
+                out=h_t[:, cols], in0=gate[:, half_cols(GATE_O, i)], in1=c_norm[:, cols]
+            )
+            nc.sync.dma_start(out=out_0[:, cols], in_=h_t[:, cols])

@@ -28,6 +28,14 @@ X_LOADS = 4
 BN_STATS = 6
 LATE_PASSES = 2
 EARLY_PASSES = IH_PASSES - LATE_PASSES
+HALVES = 2
+UNITS = (
+    (GATE_O, 0, H),
+    (GATE_F, 0, H),
+    (GATE_I, 0, H),
+    (GATE_G, 0, H // 2),
+    (GATE_G, H // 2, H // 2),
+)
 
 FLOPS = 2 * P * (IN + H) * GATES * H
 
@@ -69,6 +77,7 @@ def tile_layernormlstmcell_k_kernel(
         nc.vector.memset(warm[:], 0.0)
         nc.vector.memset(neg_half[:], -0.5)
         make_identity(nc, ident[:])
+        minus_ident = keep.tile([P, P], F32)
 
         plane_tiles = IH_PASSES // PLANES_IN_TILE + 1
         planes = keep.tile([P, plane_tiles, GATES * H], U8, align_bytes=64)
@@ -81,6 +90,7 @@ def tile_layernormlstmcell_k_kernel(
         vec_rows = keep.tile([P, H], BF16)
         nc.vector.memset(vec_rows[:].bitcast(I32), 0)
         nc.vector.tensor_copy(out=ident_bf[:], in_=ident[:])
+        nc.vector.tensor_scalar_mul(out=minus_ident[:], in0=ident[:], scalar1=-1.0)
 
         x_sb = keep.tile([P, IN], BF16)
         x_piece = IN // X_LOADS
@@ -139,13 +149,13 @@ def tile_layernormlstmcell_k_kernel(
             w_early.append(w_pass)
         w_late = []
         late_bytes = W_ih_words[EARLY_PASSES:IH_PASSES].rearrange("g p n t -> p g (n t)")
-        for n in range(GATES):
-            w_gate = keep.tile([P, LATE_PASSES, H], I32, name="w_gate%d" % n, align_bytes=64)
+        for unit, (n, first, width) in enumerate(UNITS):
+            w_unit = keep.tile([P, LATE_PASSES, width], I32, name="w_unit%d" % unit, align_bytes=64)
+            byte = PACK * (H * n + first)
             nc.sync.dma_start(
-                out=w_gate[:],
-                in_=late_bytes[:, :, PACK * H * n : PACK * H * (n + 1)].bitcast(I32),
+                out=w_unit[:], in_=late_bytes[:, :, byte : byte + PACK * width].bitcast(I32)
             )
-            w_late.append(w_gate)
+            w_late.append(w_unit)
 
         act_codes = keep.tile([P, (IH_PASSES + 1) * P], U32, align_bytes=64)
         act_scales = keep.tile([P, (IH_PASSES + 1) * P], U8, align_bytes=64)
@@ -185,28 +195,35 @@ def tile_layernormlstmcell_k_kernel(
             return summed
 
         gamma_hh_all = keep.tile([P, GATES * H], BF16)
-        gamma_ih_all = keep.tile([P, GATES * H], BF16)
+        gamma_ih_all = keep.tile([P, (GATES - 1) * H], BF16)
         hh_term = keep.tile([P, GATES * H], F32)
         for n in range(GATES):
             nc.scalar.copy(out=gamma_hh_all[:, gate_cols(n)], in_=spread_rows([row_gamma_hh + n])[:])
             nc.vector.tensor_copy(
                 out=hh_term[:, gate_cols(n)], in_=spread_rows([row_beta_ih + n, row_beta_hh + n])[:]
             )
-        for n in range(GATES):
-            if n % 2 == 0:
-                nc.scalar.copy(out=gamma_ih_all[:, gate_cols(n)], in_=spread_rows([row_gamma_ih + n])[:])
+        gamma_o = keep.tile([P, H], F32)
+        nc.scalar.copy(out=gamma_o[:], in_=spread_rows([row_gamma_ih + GATE_O])[:])
+        for n in (GATE_I, GATE_F, GATE_G):
+            gamma_bank = spread_rows([row_gamma_ih + n])
+            if n == GATE_F:
+                nc.scalar.copy(out=gamma_ih_all[:, gate_cols(n)], in_=gamma_bank[:])
             else:
-                nc.vector.tensor_copy(
-                    out=gamma_ih_all[:, gate_cols(n)], in_=spread_rows([row_gamma_ih + n])[:]
-                )
+                nc.vector.tensor_copy(out=gamma_ih_all[:, gate_cols(n)], in_=gamma_bank[:])
+
+        def new_stats(runs, columns, label):
+            stats = keep.tile([P, runs + 1, BN_STATS], F32, name="stats_" + label)
+            nc.vector.memset(stats[:, runs, :], 0.0)
+            nc.vector.tensor_scalar_mul(
+                out=stats[:, runs, 2:3], in0=neg_half[:], scalar1=-2.0 * columns * EPS
+            )
+            return stats
 
         def mean_and_inverse_std(stats, label):
             mean_var = keep.tile([P, 2], F32, name="mean_var_" + label)
-            var_eps = keep.tile([P, 1], F32, name="var_eps_" + label)
             inv_std = keep.tile([P, 1], F32, name="inv_std_" + label)
             nc.vector.bn_aggr(out=mean_var[:], in_=stats[:].rearrange("p r s -> p (r s)"))
-            nc.vector.tensor_scalar_add(out=var_eps[:], in0=mean_var[:, 1:2], scalar1=EPS)
-            nc.gpsimd.tensor_tensor(out=inv_std[:], in0=var_eps[:], in1=neg_half[:], op=ALU.pow)
+            nc.gpsimd.tensor_tensor(out=inv_std[:], in0=mean_var[:, 1:2], in1=neg_half[:], op=ALU.pow)
             return mean_var[:, 0:1], inv_std[:]
 
         def centre(out, in_, mean, gamma):
@@ -222,7 +239,7 @@ def tile_layernormlstmcell_k_kernel(
         gate = keep.tile([P, GATES * H], F32)
 
         hh_cols = slice(P * HH_PASS, P * (HH_PASS + 1))
-        hh_stats = keep.tile([P, GATES, BN_STATS], F32)
+        hh_stats = new_stats(GATES, GATES * H, "hh")
         hh_acc = []
         for n in range(GATES):
             acc = lent_banks.tile([P, H], F32, name="hh_acc%d" % n, tag="lent")
@@ -249,49 +266,78 @@ def tile_layernormlstmcell_k_kernel(
         beta_c_all = spread_rows([row_beta_c])
 
         ih_acc = []
-        for n in range(GATES):
-            acc = ih_banks.tile([P, H], F32, name="ih_acc%d" % n)
+        for unit in range(len(UNITS)):
+            if unit < GATES:
+                acc = ih_banks.tile([P, H], F32, name="ih_acc%d" % unit)
+            else:
+                acc = lent_banks.tile([P, H], F32, name="ih_acc%d" % unit, tag="lent")
             ih_acc.append(acc)
 
-        def ih_pass(n, g, words):
+        def ih_pass(unit, g, words):
+            n, first, width = UNITS[unit]
             plane_tile, place = divmod(g, PLANES_IN_TILE)
             cols = slice(P * g, P * (g + 1))
             nc.tensor.matmul_mx(
-                out=ih_acc[n][:],
+                out=ih_acc[unit][:, :width],
                 lhsT=act_codes[:, cols].bitcast(FP8X4),
                 lhsT_scale=act_scales[:, cols],
                 rhs=words.bitcast(FP8X4),
-                rhs_scale=planes[4 * place : P, plane_tile, gate_cols(n)],
+                rhs_scale=planes[4 * place : P, plane_tile, H * n + first : H * n + first + width],
                 start=(g == 0),
                 stop=(g == IH_PASSES - 1),
             )
 
         for g in range(EARLY_PASSES):
-            for n in range(GATES):
-                ih_pass(n, g, w_early[g][:, gate_cols(n)])
-        ih_stats = keep.tile([P, GATES, BN_STATS], F32)
-        for n in range(GATES):
+            for unit, (n, first, width) in enumerate(UNITS):
+                ih_pass(unit, g, w_early[g][:, H * n + first : H * n + first + width])
+        ih_stats = new_stats(len(UNITS), GATES * H, "ih")
+        c_stats = new_stats(HALVES, H, "c")
+        u_o = keep.tile([P, H], F32)
+        for unit, (n, first, width) in enumerate(UNITS):
             for late in range(LATE_PASSES):
-                ih_pass(n, EARLY_PASSES + late, w_late[n][:, late, :])
-            nc.vector.bn_stats(out=ih_stats[:, n, :], in_=ih_acc[n][:])
+                ih_pass(unit, EARLY_PASSES + late, w_late[unit][:, late, :])
+            nc.vector.bn_stats(out=ih_stats[:, unit, :], in_=ih_acc[unit][:, :width])
+            if n == GATE_O:
+                nc.vector.tensor_mul(out=u_o[:], in0=ih_acc[unit][:], in1=gamma_o[:])
 
-        halves = 2
-        half = H // halves
+        half = H // HALVES
 
         def half_cols(n, i):
             return slice(H * n + half * i, H * n + half * (i + 1))
 
         ih_mean, ih_inv_std = mean_and_inverse_std(ih_stats, "ih")
 
+        mean_inv_std = keep.tile([P, 1], F32)
+        nc.gpsimd.tensor_tensor(out=mean_inv_std[:], in0=ih_mean, in1=ih_inv_std, op=ALU.mult)
+        diag_inv_std = keep.tile([P, P], F32)
+        diag_mean = keep.tile([P, P], F32)
+        o_sum = lent_banks.tile([P, H], F32, tag="lent")
+
+        def o_product(lhsT, rhs, start, stop):
+            nc.tensor.matmul(out=o_sum[:], lhsT=lhsT, rhs=rhs, start=start, stop=stop)
+
+        o_product(ident[:], hh_term[:, gate_cols(GATE_O)], True, False)
+        nc.scalar.activation(out=diag_inv_std[:], in_=ident[:], func=ACT.Copy, scale=ih_inv_std)
+        nc.scalar.activation(
+            out=diag_mean[:], in_=minus_ident[:], func=ACT.Copy, scale=mean_inv_std[:]
+        )
+        o_product(diag_inv_std[:], u_o[:], False, False)
+        o_product(diag_mean[:], gamma_o[:], False, True)
+
         def centre_gate(n):
-            for i in range(halves):
-                cols = half_cols(n, i)
-                centre(
-                    gate[:, cols], ih_acc[n][:, half_cols(0, i)], ih_mean, gamma_ih_all[:, cols]
-                )
+            for unit, (gate_of_unit, first, width) in enumerate(UNITS):
+                if gate_of_unit == n:
+                    for col in range(0, width, half):
+                        cols = slice(H * n + first + col, H * n + first + col + half)
+                        centre(
+                            gate[:, cols],
+                            ih_acc[unit][:, col : col + half],
+                            ih_mean,
+                            gamma_ih_all[:, cols],
+                        )
 
         def finish_gate(n, func):
-            for i in range(halves):
+            for i in range(HALVES):
                 cols = half_cols(n, i)
                 scale_and_add(gate[:, cols], gate[:, cols], ih_inv_std, hh_term[:, cols])
                 nc.scalar.activation(out=gate[:, cols], in_=gate[:, cols], func=func)
@@ -306,37 +352,38 @@ def tile_layernormlstmcell_k_kernel(
         new_part = keep.tile([P, H], F32)
         kept_part = keep.tile([P, H], F32)
         c_t = keep.tile([P, H], F32)
-        c_stats = keep.tile([P, halves, BN_STATS], F32)
-        for i in range(halves):
+        for i in range(HALVES):
             cols = half_cols(0, i)
             nc.vector.tensor_mul(
                 out=new_part[:, cols], in0=gate[:, half_cols(GATE_I, i)], in1=gate[:, half_cols(GATE_G, i)]
             )
-        for i in range(halves):
+        for i in range(HALVES):
             cols = half_cols(0, i)
             nc.vector.tensor_mul(
                 out=kept_part[:, cols], in0=gate[:, half_cols(GATE_F, i)], in1=c_sb[:, cols]
             )
-        for i in range(halves):
+        for i in range(HALVES):
             cols = half_cols(0, i)
             nc.vector.tensor_add(out=c_t[:, cols], in0=new_part[:, cols], in1=kept_part[:, cols])
         nc.sync.dma_start(out=out_1, in_=c_t[:])
 
-        for i in range(halves):
+        for i in range(HALVES):
             nc.vector.bn_stats(out=c_stats[:, i, :], in_=c_t[:, half_cols(0, i)])
         c_mean, c_inv_std = mean_and_inverse_std(c_stats, "c")
         c_norm = keep.tile([P, H], F32)
         h_t = keep.tile([P, H], F32)
-        centre_gate(GATE_O)
-        for i in range(halves):
+        for i in range(HALVES):
+            nc.scalar.activation(
+                out=gate[:, half_cols(GATE_O, i)], in_=o_sum[:, half_cols(0, i)], func=ACT.Sigmoid
+            )
+        for i in range(HALVES):
             cols = half_cols(0, i)
             centre(c_norm[:, cols], c_t[:, cols], c_mean, gamma_c_all[:, cols])
-        finish_gate(GATE_O, ACT.Sigmoid)
-        for i in range(halves):
+        for i in range(HALVES):
             cols = half_cols(0, i)
             scale_and_add(c_norm[:, cols], c_norm[:, cols], c_inv_std, beta_c_all[:, cols])
             nc.scalar.activation(out=c_norm[:, cols], in_=c_norm[:, cols], func=ACT.Tanh)
-        for i in range(halves):
+        for i in range(HALVES):
             cols = half_cols(0, i)
             nc.vector.tensor_mul(
                 out=h_t[:, cols], in0=gate[:, half_cols(GATE_O, i)], in1=c_norm[:, cols]

from contextlib import ExitStack

import concourse.mybir as mybir
from concourse.masks import make_identity

F32 = mybir.dt.float32
BF16 = mybir.dt.bfloat16
I32 = mybir.dt.int32
U32 = mybir.dt.uint32
U8 = mybir.dt.uint8
FP8X4 = mybir.dt.float8_e4m3fn_x4
ALU = mybir.AluOpType
ACT = mybir.ActivationFunctionType

P = 128
PACK = 4
K_PASS = P * PACK
IN = 8192
H = 512
GATES = 4
GATE_I, GATE_F, GATE_G, GATE_O = 0, 1, 2, 3
EPS = 1e-5
IH_PASSES = IN // K_PASS
HH_PASS = IH_PASSES
WORDS = K_PASS // 2
PLANES_IN_TILE = 4
X_LOADS = 4
BN_STATS = 6
LATE_PASSES = 2
EARLY_PASSES = IH_PASSES - LATE_PASSES
HALVES = 2
UNITS = (
    (GATE_O, 0, H),
    (GATE_F, 0, H),
    (GATE_I, 0, H),
    (GATE_G, 0, H // 2),
    (GATE_G, H // 2, H // 2),
)

FLOPS = 2 * P * (IN + H) * GATES * H


def gate_cols(n):
    return slice(H * n, H * (n + 1))


def tile_layernormlstmcell_k_kernel(
    tc,
    x,
    h_prev,
    c_prev,
    W_ih_words,
    W_ih_scales,
    W_hh_words,
    W_hh_scales,
    gamma_ih,
    beta_ih,
    gamma_hh,
    beta_hh,
    gamma_c,
    beta_c,
    out_0,
    out_1,
):
    nc = tc.nc
    with ExitStack() as ctx:
        keep = ctx.enter_context(tc.tile_pool(name="keep", bufs=1))
        stage = ctx.enter_context(tc.tile_pool(name="stage", bufs=2))
        ih_banks = ctx.enter_context(tc.psum_pool(name="ih_banks", bufs=1))
        lent_banks = ctx.enter_context(tc.psum_pool(name="lent_banks", bufs=4))
        ctx.enter_context(tc.manual_schedule())

        warm = keep.tile([P, 1], F32)
        neg_half = keep.tile([P, 1], F32)
        ident_bf = keep.tile([P, P], BF16)
        ident = keep.tile([P, P], F32)
        nc.vector.memset(warm[:], 0.0)
        nc.vector.memset(neg_half[:], -0.5)
        make_identity(nc, ident[:])
        minus_ident = keep.tile([P, P], F32)

        plane_tiles = IH_PASSES // PLANES_IN_TILE + 1
        planes = keep.tile([P, plane_tiles, GATES * H], U8, align_bytes=64)
        nc.vector.memset(planes[:, plane_tiles - 1, :].bitcast(I32), 0)
        for j in range(plane_tiles - 1):
            nc.vector.memset(planes[:, j, :].bitcast(I32), 0)

        row_gamma_hh, row_gamma_ih, row_beta_ih, row_beta_hh = 0, GATES, 2 * GATES, 3 * GATES
        row_gamma_c, row_beta_c = 4 * GATES, 4 * GATES + 1
        vec_rows = keep.tile([P, H], BF16)
        nc.vector.memset(vec_rows[:].bitcast(I32), 0)
        nc.vector.tensor_copy(out=ident_bf[:], in_=ident[:])
        nc.vector.tensor_scalar_mul(out=minus_ident[:], in0=ident[:], scalar1=-1.0)

        x_sb = keep.tile([P, IN], BF16)
        x_piece = IN // X_LOADS
        for i in range(X_LOADS):
            cols = slice(x_piece * i, x_piece * (i + 1))
            nc.sync.dma_start(out=x_sb[:, cols], in_=x[:, cols])

        h_sb = keep.tile([P, H], BF16)
        c_sb = keep.tile([P, H], BF16)
        nc.scalar.dma_start(out=h_sb[:], in_=h_prev)
        nc.scalar.activation(out=warm[:], in_=warm[:], func=ACT.Sigmoid)
        for vector, row in (
            (gamma_hh, row_gamma_hh),
            (gamma_ih, row_gamma_ih),
            (beta_ih, row_beta_ih),
            (beta_hh, row_beta_hh),
            (gamma_c, row_gamma_c),
            (beta_c, row_beta_c),
        ):
            rows = vector.shape[0] // H
            nc.scalar.dma_start(
                out=vec_rows[row : row + rows, :], in_=vector.rearrange("(r n) -> r n", r=rows)
            )
        nc.scalar.dma_start(out=c_sb[:], in_=c_prev)

        def load_hh_scales():
            for Q in range(4):
                nc.gpsimd.dma_start(
                    out=planes[32 * Q : 32 * Q + 4, plane_tiles - 1, :].bitcast(F32),
                    in_=W_hh_scales[0, 4 * Q : 4 * Q + 4, :].bitcast(F32),
                )

        def load_ih_scales(j):
            for Q in range(4):
                nc.gpsimd.dma_start(
                    out=planes[32 * Q : 32 * Q + 16, j, :].bitcast(F32),
                    in_=W_ih_scales[
                        PLANES_IN_TILE * j : PLANES_IN_TILE * (j + 1), 4 * Q : 4 * Q + 4, :
                    ].bitcast(F32),
                )

        load_hh_scales()
        for j in range(IH_PASSES // PLANES_IN_TILE):
            load_ih_scales(j)

        w_hh = keep.tile([P, GATES * H], I32, align_bytes=64)
        nc.sync.dma_start(
            out=w_hh[:], in_=W_hh_words[0].rearrange("p n t -> p (n t)").bitcast(I32)
        )
        w_early = []
        for g in range(EARLY_PASSES):
            w_pass = keep.tile([P, GATES * H], I32, name="w_pass%d" % g, align_bytes=64)
            nc.sync.dma_start(
                out=w_pass[:], in_=W_ih_words[g].rearrange("p n t -> p (n t)").bitcast(I32)
            )
            w_early.append(w_pass)
        w_late = []
        late_bytes = W_ih_words[EARLY_PASSES:IH_PASSES].rearrange("g p n t -> p g (n t)")
        for unit, (n, first, width) in enumerate(UNITS):
            w_unit = keep.tile([P, LATE_PASSES, width], I32, name="w_unit%d" % unit, align_bytes=64)
            byte = PACK * (H * n + first)
            nc.sync.dma_start(
                out=w_unit[:], in_=late_bytes[:, :, byte : byte + PACK * width].bitcast(I32)
            )
            w_late.append(w_unit)

        act_codes = keep.tile([P, (IH_PASSES + 1) * P], U32, align_bytes=64)
        act_scales = keep.tile([P, (IH_PASSES + 1) * P], U8, align_bytes=64)

        def quantise_passes(rows, first_pass, passes):
            words = rows.bitcast(F32)
            turned = lent_banks.tile([P, passes, 2, P], F32, tag="lent")
            for g in range(passes):
                for u in range(2):
                    nc.tensor.transpose(
                        turned[:, g, u, :], words[:, WORDS * g + u : WORDS * (g + 1) : 2], ident[:]
                    )
            grouped = stage.tile([P, passes * K_PASS], BF16, tag="grouped", align_bytes=64)
            nc.scalar.copy(
                out=grouped[:].bitcast(F32).rearrange("p (g b u) -> p g b u", g=passes, u=2),
                in_=turned[:].rearrange("p g u b -> p g b u"),
            )
            cols = slice(P * first_pass, P * (first_pass + passes))
            nc.vector.quantize_mx(
                out=act_codes[:, cols].bitcast(FP8X4), scales=act_scales[:, cols], in_=grouped[:]
            )

        quantise_passes(h_sb[:], HH_PASS, 1)
        for g in range(0, IH_PASSES, 2):
            quantise_passes(x_sb[:, K_PASS * g : K_PASS * (g + 2)], g, 2)

        def spread_rows(rows_to_add):
            summed = lent_banks.tile([P, H], F32, name="summed", tag="lent")
            for i, r in enumerate(rows_to_add):
                nc.tensor.matmul(
                    out=summed[:],
                    lhsT=ident_bf[:, r : r + 1].to_broadcast([P, P]),
                    rhs=vec_rows[:],
                    start=(i == 0),
                    stop=(i == len(rows_to_add) - 1),
                )
            return summed

        gamma_hh_all = keep.tile([P, GATES * H], BF16)
        gamma_ih_all = keep.tile([P, (GATES - 1) * H], BF16)
        hh_term = keep.tile([P, GATES * H], F32)
        for n in range(GATES):
            nc.scalar.copy(out=gamma_hh_all[:, gate_cols(n)], in_=spread_rows([row_gamma_hh + n])[:])
            nc.vector.tensor_copy(
                out=hh_term[:, gate_cols(n)], in_=spread_rows([row_beta_ih + n, row_beta_hh + n])[:]
            )
        gamma_o = keep.tile([P, H], F32)
        nc.scalar.copy(out=gamma_o[:], in_=spread_rows([row_gamma_ih + GATE_O])[:])
        for n in (GATE_I, GATE_F, GATE_G):
            gamma_bank = spread_rows([row_gamma_ih + n])
            if n == GATE_F:
                nc.scalar.copy(out=gamma_ih_all[:, gate_cols(n)], in_=gamma_bank[:])
            else:
                nc.vector.tensor_copy(out=gamma_ih_all[:, gate_cols(n)], in_=gamma_bank[:])

        def new_stats(runs, columns, label):
            stats = keep.tile([P, runs + 1, BN_STATS], F32, name="stats_" + label)
            nc.vector.memset(stats[:, runs, :], 0.0)
            nc.vector.tensor_scalar_mul(
                out=stats[:, runs, 2:3], in0=neg_half[:], scalar1=-2.0 * columns * EPS
            )
            return stats

        def mean_and_inverse_std(stats, label):
            mean_var = keep.tile([P, 2], F32, name="mean_var_" + label)
            inv_std = keep.tile([P, 1], F32, name="inv_std_" + label)
            nc.vector.bn_aggr(out=mean_var[:], in_=stats[:].rearrange("p r s -> p (r s)"))
            nc.gpsimd.tensor_tensor(out=inv_std[:], in0=mean_var[:, 1:2], in1=neg_half[:], op=ALU.pow)
            return mean_var[:, 0:1], inv_std[:]

        def centre(out, in_, mean, gamma):
            nc.vector.scalar_tensor_tensor(
                out=out, in0=in_, scalar=mean, in1=gamma, op0=ALU.subtract, op1=ALU.mult
            )

        def scale_and_add(out, in_, inv_std, addend):
            nc.vector.scalar_tensor_tensor(
                out=out, in0=in_, scalar=inv_std, in1=addend, op0=ALU.mult, op1=ALU.add
            )

        gate = keep.tile([P, GATES * H], F32)

        hh_cols = slice(P * HH_PASS, P * (HH_PASS + 1))
        hh_stats = new_stats(GATES, GATES * H, "hh")
        hh_acc = []
        for n in range(GATES):
            acc = lent_banks.tile([P, H], F32, name="hh_acc%d" % n, tag="lent")
            nc.tensor.matmul_mx(
                out=acc[:],
                lhsT=act_codes[:, hh_cols].bitcast(FP8X4),
                lhsT_scale=act_scales[:, hh_cols],
                rhs=w_hh[:, gate_cols(n)].bitcast(FP8X4),
                rhs_scale=planes[:, plane_tiles - 1, gate_cols(n)],
                start=True,
                stop=True,
            )
            nc.vector.bn_stats(out=hh_stats[:, n, :], in_=acc[:])
            hh_acc.append(acc)
        hh_mean, hh_inv_std = mean_and_inverse_std(hh_stats, "hh")
        for n in range(GATES):
            centre(gate[:, gate_cols(n)], hh_acc[n][:], hh_mean, gamma_hh_all[:, gate_cols(n)])
        for n in range(GATES):
            scale_and_add(
                hh_term[:, gate_cols(n)], gate[:, gate_cols(n)], hh_inv_std, hh_term[:, gate_cols(n)]
            )

        gamma_c_all = spread_rows([row_gamma_c])
        beta_c_all = spread_rows([row_beta_c])

        ih_acc = []
        for unit in range(len(UNITS)):
            if unit < GATES:
                acc = ih_banks.tile([P, H], F32, name="ih_acc%d" % unit)
            else:
                acc = lent_banks.tile([P, H], F32, name="ih_acc%d" % unit, tag="lent")
            ih_acc.append(acc)

        def ih_pass(unit, g, words):
            n, first, width = UNITS[unit]
            plane_tile, place = divmod(g, PLANES_IN_TILE)
            cols = slice(P * g, P * (g + 1))
            nc.tensor.matmul_mx(
                out=ih_acc[unit][:, :width],
                lhsT=act_codes[:, cols].bitcast(FP8X4),
                lhsT_scale=act_scales[:, cols],
                rhs=words.bitcast(FP8X4),
                rhs_scale=planes[4 * place : P, plane_tile, H * n + first : H * n + first + width],
                start=(g == 0),
                stop=(g == IH_PASSES - 1),
            )

        for g in range(EARLY_PASSES):
            for unit, (n, first, width) in enumerate(UNITS):
                ih_pass(unit, g, w_early[g][:, H * n + first : H * n + first + width])
        ih_stats = new_stats(len(UNITS), GATES * H, "ih")
        c_stats = new_stats(HALVES, H, "c")
        u_o = keep.tile([P, H], F32)
        for unit, (n, first, width) in enumerate(UNITS):
            for late in range(LATE_PASSES):
                ih_pass(unit, EARLY_PASSES + late, w_late[unit][:, late, :])
            nc.vector.bn_stats(out=ih_stats[:, unit, :], in_=ih_acc[unit][:, :width])
            if n == GATE_O:
                nc.vector.tensor_mul(out=u_o[:], in0=ih_acc[unit][:], in1=gamma_o[:])

        half = H // HALVES

        def half_cols(n, i):
            return slice(H * n + half * i, H * n + half * (i + 1))

        ih_mean, ih_inv_std = mean_and_inverse_std(ih_stats, "ih")

        mean_inv_std = keep.tile([P, 1], F32)
        nc.gpsimd.tensor_tensor(out=mean_inv_std[:], in0=ih_mean, in1=ih_inv_std, op=ALU.mult)
        diag_inv_std = keep.tile([P, P], F32)
        diag_mean = keep.tile([P, P], F32)
        o_sum = lent_banks.tile([P, H], F32, tag="lent")

        def o_product(lhsT, rhs, start, stop):
            nc.tensor.matmul(out=o_sum[:], lhsT=lhsT, rhs=rhs, start=start, stop=stop)

        o_product(ident[:], hh_term[:, gate_cols(GATE_O)], True, False)
        nc.scalar.activation(out=diag_inv_std[:], in_=ident[:], func=ACT.Copy, scale=ih_inv_std)
        nc.scalar.activation(
            out=diag_mean[:], in_=minus_ident[:], func=ACT.Copy, scale=mean_inv_std[:]
        )
        o_product(diag_inv_std[:], u_o[:], False, False)
        o_product(diag_mean[:], gamma_o[:], False, True)

        def centre_gate(n):
            for unit, (gate_of_unit, first, width) in enumerate(UNITS):
                if gate_of_unit == n:
                    for col in range(0, width, half):
                        cols = slice(H * n + first + col, H * n + first + col + half)
                        centre(
                            gate[:, cols],
                            ih_acc[unit][:, col : col + half],
                            ih_mean,
                            gamma_ih_all[:, cols],
                        )

        def finish_gate(n, func):
            for i in range(HALVES):
                cols = half_cols(n, i)
                scale_and_add(gate[:, cols], gate[:, cols], ih_inv_std, hh_term[:, cols])
                nc.scalar.activation(out=gate[:, cols], in_=gate[:, cols], func=func)

        centre_gate(GATE_G)
        centre_gate(GATE_I)
        centre_gate(GATE_F)
        finish_gate(GATE_G, ACT.Tanh)
        finish_gate(GATE_I, ACT.Sigmoid)
        finish_gate(GATE_F, ACT.Sigmoid)

        new_part = keep.tile([P, H], F32)
        kept_part = keep.tile([P, H], F32)
        c_t = keep.tile([P, H], F32)
        for i in range(HALVES):
            cols = half_cols(0, i)
            nc.vector.tensor_mul(
                out=new_part[:, cols], in0=gate[:, half_cols(GATE_I, i)], in1=gate[:, half_cols(GATE_G, i)]
            )
        for i in range(HALVES):
            cols = half_cols(0, i)
            nc.vector.tensor_mul(
                out=kept_part[:, cols], in0=gate[:, half_cols(GATE_F, i)], in1=c_sb[:, cols]
            )
        for i in range(HALVES):
            cols = half_cols(0, i)
            nc.vector.tensor_add(out=c_t[:, cols], in0=new_part[:, cols], in1=kept_part[:, cols])
        nc.sync.dma_start(out=out_1, in_=c_t[:])

        for i in range(HALVES):
            nc.vector.bn_stats(out=c_stats[:, i, :], in_=c_t[:, half_cols(0, i)])
        c_mean, c_inv_std = mean_and_inverse_std(c_stats, "c")
        c_norm = keep.tile([P, H], F32)
        h_t = keep.tile([P, H], F32)
        for i in range(HALVES):
            nc.scalar.activation(
                out=gate[:, half_cols(GATE_O, i)], in_=o_sum[:, half_cols(0, i)], func=ACT.Sigmoid
            )
        for i in range(HALVES):
            cols = half_cols(0, i)
            centre(c_norm[:, cols], c_t[:, cols], c_mean, gamma_c_all[:, cols])
        for i in range(HALVES):
            cols = half_cols(0, i)
            scale_and_add(c_norm[:, cols], c_norm[:, cols], c_inv_std, beta_c_all[:, cols])
            nc.scalar.activation(out=c_norm[:, cols], in_=c_norm[:, cols], func=ACT.Tanh)
        for i in range(HALVES):
            cols = half_cols(0, i)
            nc.vector.tensor_mul(
                out=h_t[:, cols], in0=gate[:, half_cols(GATE_O, i)], in1=c_norm[:, cols]
            )
            nc.sync.dma_start(out=out_0[:, cols], in_=h_t[:, cols])
